import numpy as np
import ml_dtypes

BF16 = ml_dtypes.bfloat16


def bf(x):
    return np.asarray(x, np.float32).astype(BF16)


def f32(x):
    return np.asarray(x, np.float32)


def f64(x):
    return np.asarray(x).astype(np.float64)


def striped(idx):
    return np.tile(idx.reshape(-1, 16).T, (8, 1))


C, S, N, M = 256, 256, 128, 128


def silu(v):
    return v / (1.0 + np.exp(-v))


def setup_inputs():
    return {"x": f32(np.random.standard_normal((C, S))), "lig": f32(np.random.standard_normal((C, N))), "w1": bf(np.random.uniform(-1.0, 1.0, (C, M)) / np.sqrt(C)), "b1": f32(0.1 * np.random.standard_normal((M, 1))), "offs": striped(np.random.permutation(np.tile(np.arange(S), 2))[:N])}


def reference(x, lig, w1, b1, offs):
    idx = offs[:16].T.reshape(-1)
    s = f64(x)[:, idx] + f64(lig)
    return silu(f64(w1).T @ s + f64(b1))

@@ -1,0 +1,80 @@
+import concourse.mybir as mybir
+
+F32 = mybir.dt.float32
+BF16 = mybir.dt.bfloat16
+U16 = mybir.dt.uint16
+
+P = 128
+C = 256
+S = 256
+N = 128
+M = 128
+BLOCKS = C // P
+HALF = N // 2
+BANK = 512
+IDLE_MATMULS = 6
+
+FLOPS = 2 * C * M * N
+
+
+def tile_hiddenedgedistancemlp_kernel(tc, x, lig, w1, b1, offs, out):
+    nc = tc.nc
+    x_blocks = x.rearrange("(p b) s -> b p s", b=BLOCKS)
+    lig_rows = lig.rearrange("(p b) n -> p (b n)", b=BLOCKS)
+    w1_rows = w1.rearrange("(p b) m -> p (b m)", b=BLOCKS)
+
+    with (
+        tc.tile_pool(name="held", bufs=1) as held,
+        tc.psum_pool(name="psum", bufs=1) as psum,
+    ):
+        offsets = held.tile([P, N // 16], U16, name="offsets")
+        nc.sync.dma_start(offsets[:], offs)
+
+        window0 = held.tile([P, S], F32, name="window0")
+        nc.sync.dma_start(window0[:], x_blocks[0])
+        ligands = held.tile([P, BLOCKS * N], F32, name="ligands")
+        nc.scalar.dma_start(ligands[:], lig_rows)
+        window1 = held.tile([P, S], F32, name="window1")
+        nc.scalar.dma_start(window1[:], x_blocks[1])
+        weights = held.tile([P, BLOCKS * M], BF16, name="weights")
+        nc.sync.dma_start(weights[:], w1_rows)
+        bias = held.tile([M, 1], F32, name="bias")
+        nc.sync.dma_start(bias[:], b1)
+
+        warm = held.tile([P, 1], F32, name="warm")
+        nc.vector.memset(warm[:], 0.0)
+        nc.scalar.activation(warm[:], warm[:], mybir.ActivationFunctionType.Silu)
+
+        zeros = held.tile([P, BANK], BF16, name="zeros")
+        nc.vector.memset(zeros[:], 0.0)
+        unread = psum.tile([P, BANK], F32, name="unread")
+        for i in range(IDLE_MATMULS):
+            nc.tensor.matmul(unread[:], zeros[:, 0:P], zeros[:], start=True, stop=True)
+
+        summed0 = held.tile([P, N], F32, name="summed0")
+        nc.vector.tensor_tensor(summed0[:], window0[:].indirect(offsets[:]), ligands[:, 0:N], mybir.AluOpType.add)
+        rounded0 = held.tile([P, N], BF16, name="rounded0")
+        nc.scalar.copy(rounded0[:], summed0[:])
+
+        summed1 = [held.tile([P, HALF], F32, name=f"summed1_{h}") for h in range(2)]
+        for h in range(2):
+            nc.vector.tensor_tensor(
+                summed1[h][:],
+                window1[:].indirect(offsets[:, h * HALF // 16 : (h + 1) * HALF // 16]),
+                ligands[:, N + h * HALF : N + (h + 1) * HALF],
+                mybir.AluOpType.add,
+            )
+        hidden = [psum.tile([M, BANK], F32, name=f"hidden{h}") for h in range(2)]
+        for h in range(2):
+            nc.tensor.matmul(
+                hidden[h][:, 0:HALF], weights[:, 0:M], rounded0[:, h * HALF : (h + 1) * HALF], start=True, stop=False
+            )
+        for h in range(2):
+            rounded1 = held.tile([P, HALF], BF16, name=f"rounded1_{h}")
+            nc.vector.tensor_copy(rounded1[:], summed1[h][:])
+            nc.tensor.matmul(hidden[h][:, 0:HALF], weights[:, M : 2 * M], rounded1[:], start=False, stop=True)
+            activated = held.tile([M, HALF], F32, name=f"activated{h}")
+            nc.scalar.activation(
+                activated[:], hidden[h][:, 0:HALF], mybir.ActivationFunctionType.Silu, bias=bias[:]
+            )
+            nc.sync.dma_start(out[:, h * HALF : (h + 1) * HALF], activated[:])

@@ -12,7 +12,6 @@ M = 128
 BLOCKS = C // P
 HALF = N // 2
 BANK = 512
-IDLE_MATMULS = 6
 
 FLOPS = 2 * C * M * N
 
@@ -27,11 +26,10 @@ def tile_hiddenedgedistancemlp_kernel(tc, x, lig, w1, b1, offs, out):
         tc.tile_pool(name="held", bufs=1) as held,
         tc.psum_pool(name="psum", bufs=1) as psum,
     ):
-        offsets = held.tile([P, N // 16], U16, name="offsets")
-        nc.sync.dma_start(offsets[:], offs)
-
         window0 = held.tile([P, S], F32, name="window0")
         nc.sync.dma_start(window0[:], x_blocks[0])
+        offsets = held.tile([P, N // 16], U16, name="offsets")
+        nc.sync.dma_start(offsets[:], offs)
         ligands = held.tile([P, BLOCKS * N], F32, name="ligands")
         nc.scalar.dma_start(ligands[:], lig_rows)
         window1 = held.tile([P, S], F32, name="window1")
@@ -44,12 +42,6 @@ def tile_hiddenedgedistancemlp_kernel(tc, x, lig, w1, b1, offs, out):
         warm = held.tile([P, 1], F32, name="warm")
         nc.vector.memset(warm[:], 0.0)
         nc.scalar.activation(warm[:], warm[:], mybir.ActivationFunctionType.Silu)
-
-        zeros = held.tile([P, BANK], BF16, name="zeros")
-        nc.vector.memset(zeros[:], 0.0)
-        unread = psum.tile([P, BANK], F32, name="unread")
-        for i in range(IDLE_MATMULS):
-            nc.tensor.matmul(unread[:], zeros[:, 0:P], zeros[:], start=True, stop=True)
 
         summed0 = held.tile([P, N], F32, name="summed0")
         nc.vector.tensor_tensor(summed0[:], window0[:].indirect(offsets[:]), ligands[:, 0:N], mybir.AluOpType.add)

import concourse.mybir as mybir

F32 = mybir.dt.float32
BF16 = mybir.dt.bfloat16
U16 = mybir.dt.uint16

P = 128
C = 256
S = 256
N = 128
M = 128
BLOCKS = C // P
HALF = N // 2
BANK = 512

FLOPS = 2 * C * M * N


def tile_hiddenedgedistancemlp_kernel(tc, x, lig, w1, b1, offs, out):
    nc = tc.nc
    x_blocks = x.rearrange("(p b) s -> b p s", b=BLOCKS)
    lig_rows = lig.rearrange("(p b) n -> p (b n)", b=BLOCKS)
    w1_rows = w1.rearrange("(p b) m -> p (b m)", b=BLOCKS)

    with (
        tc.tile_pool(name="held", bufs=1) as held,
        tc.psum_pool(name="psum", bufs=1) as psum,
    ):
        window0 = held.tile([P, S], F32, name="window0")
        nc.sync.dma_start(window0[:], x_blocks[0])
        offsets = held.tile([P, N // 16], U16, name="offsets")
        nc.sync.dma_start(offsets[:], offs)
        ligands = held.tile([P, BLOCKS * N], F32, name="ligands")
        nc.scalar.dma_start(ligands[:], lig_rows)
        window1 = held.tile([P, S], F32, name="window1")
        nc.scalar.dma_start(window1[:], x_blocks[1])
        weights = held.tile([P, BLOCKS * M], BF16, name="weights")
        nc.sync.dma_start(weights[:], w1_rows)
        bias = held.tile([M, 1], F32, name="bias")
        nc.sync.dma_start(bias[:], b1)

        warm = held.tile([P, 1], F32, name="warm")
        nc.vector.memset(warm[:], 0.0)
        nc.scalar.activation(warm[:], warm[:], mybir.ActivationFunctionType.Silu)

        summed0 = held.tile([P, N], F32, name="summed0")
        nc.vector.tensor_tensor(summed0[:], window0[:].indirect(offsets[:]), ligands[:, 0:N], mybir.AluOpType.add)
        rounded0 = held.tile([P, N], BF16, name="rounded0")
        nc.scalar.copy(rounded0[:], summed0[:])

        summed1 = [held.tile([P, HALF], F32, name=f"summed1_{h}") for h in range(2)]
        for h in range(2):
            nc.vector.tensor_tensor(
                summed1[h][:],
                window1[:].indirect(offsets[:, h * HALF // 16 : (h + 1) * HALF // 16]),
                ligands[:, N + h * HALF : N + (h + 1) * HALF],
                mybir.AluOpType.add,
            )
        hidden = [psum.tile([M, BANK], F32, name=f"hidden{h}") for h in range(2)]
        for h in range(2):
            nc.tensor.matmul(
                hidden[h][:, 0:HALF], weights[:, 0:M], rounded0[:, h * HALF : (h + 1) * HALF], start=True, stop=False
            )
        for h in range(2):
            rounded1 = held.tile([P, HALF], BF16, name=f"rounded1_{h}")
            nc.vector.tensor_copy(rounded1[:], summed1[h][:])
            nc.tensor.matmul(hidden[h][:, 0:HALF], weights[:, M : 2 * M], rounded1[:], start=False, stop=True)
            activated = held.tile([M, HALF], F32, name=f"activated{h}")
            nc.scalar.activation(
                activated[:], hidden[h][:, 0:HALF], mybir.ActivationFunctionType.Silu, bias=bias[:]
            )
            nc.sync.dma_start(out[:, h * HALF : (h + 1) * HALF], activated[:])
